import numpy as np
import ml_dtypes


def mxq(x, axis, fmt="e4m3"):
    dtype, down = {"e4m3": (ml_dtypes.float8_e4m3fn, 7), "e5m2": (ml_dtypes.float8_e5m2, 14)}[fmt]
    v = np.moveaxis(np.asarray(x, np.float32).astype(ml_dtypes.bfloat16).astype(np.float64), axis, -1)
    blocks = v.reshape(v.shape[:-1] + (-1, 32))
    amax = np.abs(blocks).max(-1, keepdims=True)
    byte = np.maximum(np.where(amax > 0, np.frexp(amax)[1] - 1 + 127, 0) - down, 1)
    scale = np.exp2(byte - 127.0)
    codes = (blocks / scale).astype(np.float32).astype(dtype).astype(np.float64)
    return np.moveaxis((codes * scale).reshape(v.shape), -1, axis)


WIDE = False


def mx_kscale(k):
    if not WIDE:
        return np.ones(k)
    levels = np.array([10, -10, 5, -5, 0])
    a = np.random.permutation(np.resize(levels, k // 512 * 4)).reshape(k // 512, 4)
    idx = np.arange(k)
    return np.exp2(a[idx // 512, idx % 128 // 32])


BF16 = ml_dtypes.bfloat16


def bf(x):
    return np.asarray(x, np.float32).astype(BF16)


def f64(x):
    return np.asarray(x).astype(np.float64)


B, Q, K, D = 2, 4096, 512, 1024
SIG = 2.0
PMASK = 0.1


def setup_inputs():
    s = mx_kscale(D)
    q = np.random.standard_normal((B, Q, D)) * s
    k = np.random.standard_normal((B, K, D)) * (SIG / np.sqrt(D)) / s
    k[:, :, 0] = np.where(np.random.random((B, K)) < PMASK, 0.0, k[:, :, 0])
    temperature = 1.0 + 0.1 * np.random.standard_normal(1)
    bias = -(np.log(K) + SIG ** 2 / 2.0) + 0.1 * np.random.standard_normal(1)
    return {"queries": bf(q), "keys": bf(k), "temperature": bf(temperature), "bias": bf(bias)}


def reference(queries, keys, temperature, bias):
    kf = f64(keys)
    logits = mxq(f64(queries), 2, "e4m3") @ mxq(kf, 2, "e4m3").transpose(0, 2, 1)
    key_mask = (kf[:, :, 0] == 0.0)[:, None, :]
    logits = np.where(key_mask, -np.inf, logits)
    m = logits.max(-1, keepdims=True)
    e = np.exp(logits - m)
    z = e.sum(-1, keepdims=True)
    approx_max_logit = (np.log(z) + m)[:, :, 0]
    confidence = 1.0 / (1.0 + np.exp(-((approx_max_logit + f64(bias)) * f64(temperature))))
    attn = e / z
    return attn, confidence

@@ -1,0 +1,271 @@
+from contextlib import ExitStack
+
+import concourse.mybir as mybir
+from concourse.masks import make_identity
+
+F32 = mybir.dt.float32
+BF16 = mybir.dt.bfloat16
+U32 = mybir.dt.uint32
+U8 = mybir.dt.uint8
+FP8X4 = mybir.dt.float8_e4m3fn_x4
+ALU = mybir.AluOpType
+ACT = mybir.ActivationFunctionType
+AX = mybir.AxisListType
+
+P = 128
+B, Q, K, D = 2, 4096, 512, 1024
+FLOPS = 2 * B * Q * K * D
+R = 4
+TILES_B = Q // P
+CHUNKS_B = TILES_B // R
+N_TILES = B * TILES_B
+N_PAIRS = N_TILES // 2
+BIG = 2.0 ** 120
+AHEAD = 8
+
+
+def tile_contentattention_t_kernel(tc, queries, keys, temperature, bias, out_0, out_1):
+    nc = tc.nc
+    with ExitStack() as ctx:
+        const = ctx.enter_context(tc.tile_pool(name="const", bufs=1))
+        qpool = ctx.enter_context(tc.tile_pool(name="qpool", bufs=10))
+        gpool = ctx.enter_context(tc.tile_pool(name="gpool", bufs=3))
+        cpool = ctx.enter_context(tc.tile_pool(name="cpool", bufs=4))
+        opool = ctx.enter_context(tc.tile_pool(name="opool", bufs=4))
+        ps_t = ctx.enter_context(tc.psum_pool(name="ps_t", bufs=4))
+        ps_l = ctx.enter_context(tc.psum_pool(name="ps_l", bufs=4))
+
+        one = const.tile([P, 1], F32, name="one")
+        junk = const.tile([P, 1], F32, name="junk")
+        nc.vector.memset(one[:], 1.0)
+        nc.scalar.activation(out=junk[:], in_=one[:], func=ACT.Exp)
+        ident_f = const.tile([P, P], F32, name="ident_f")
+        ident_b = const.tile([P, P], BF16, name="ident_b")
+        make_identity(nc, ident_f[:])
+        make_identity(nc, ident_b[:])
+
+        k_sb = const.tile([P, B * 4 * D], BF16, name="k_sb")
+        k32 = k_sb[:].bitcast(F32)
+        zsum = const.tile([P, N_TILES], F32, name="zsum")
+        negm = const.tile([P, N_TILES], F32, name="negm")
+        rz = const.tile([P, N_TILES], F32, name="rz")
+        t_bf = const.tile([P, 1], BF16, name="t_bf")
+        b_bf = const.tile([P, 1], BF16, name="b_bf")
+        t_f = const.tile([P, 1], F32, name="t_f")
+        t_b = const.tile([P, 1], F32, name="t_b")
+
+        q_tiles = {}
+
+        def load_keys(b):
+            for h in range(2):
+                nc.sync.dma_start(
+                    out=k_sb[:, (b * 4 + 2 * h) * D : (b * 4 + 2 * h + 2) * D].rearrange("p (t d) -> p t d", t=2),
+                    in_=keys[b][2 * h * P : (2 * h + 2) * P, :].rearrange("(t p) d -> p t d", p=P),
+                )
+
+        def load_chunk(c, pieces=1):
+            b, cc = divmod(c, CHUNKS_B)
+            q_sb = qpool.tile([P, R * D], BF16, name="q_sb")
+            w = R * D // pieces
+            for h in range(pieces):
+                nc.sync.dma_start(
+                    out=q_sb[:, h * w : (h + 1) * w],
+                    in_=queries[b].rearrange("(p r) d -> p (r d)", p=P)[:, cc * R * D + h * w : cc * R * D + (h + 1) * w],
+                )
+            q_tiles[c] = q_sb
+
+        kcodes, kscl, caps = {}, {}, {}
+
+        gks = {}
+
+        def keys_cap(b):
+            capv = const.tile([P, 4], BF16, name="capv%d" % b)
+            first = k_sb[:, b * 4 * D : (b + 1) * 4 * D].rearrange("p (t d) -> p t d", t=4)[:, :, 0:1]
+            nc.vector.tensor_scalar(out=capv[:].rearrange("p (t o) -> p t o", o=1), in0=first, scalar1=0.0, scalar2=-2.0 * BIG, op0=ALU.is_equal, op1=ALU.mult)
+            nc.vector.tensor_scalar_add(out=capv[:], in0=capv[:], scalar1=BIG)
+            cap_ps = ps_t.tile([P, K], F32, name="cap_ps", tag="xt")
+            for t in range(4):
+                nc.tensor.matmul(
+                    out=cap_ps[:, t * P : (t + 1) * P],
+                    lhsT=capv[:, t : t + 1].to_broadcast([P, P]),
+                    rhs=ident_b[:],
+                    start=True,
+                    stop=True,
+                )
+            cap = const.tile([P, K], F32, name="cap%d" % b)
+            nc.scalar.copy(out=cap[:], in_=cap_ps[:])
+            caps[b] = cap
+
+        def keys_transpose(b, t, on_vector):
+            if t == 0:
+                gk = const.tile([P, 2 * K * 4], BF16, name="gk%d" % b, align_bytes=64)
+                gks[b] = gk
+            gk32 = gks[b][:].bitcast(F32).rearrange("p (g j u) -> p g j u", g=2, u=2)
+            xt = ps_t.tile([P, 2, 2, P], F32, name="xt", tag="xt")
+            for w in range(4):
+                col = (b * 4 + t) * (D // 2) + w * P
+                nc.tensor.transpose(xt[:, w // 2, w % 2, :], k32[:, col : col + P], ident_f[:])
+            dst = gk32[:, :, t * P : (t + 1) * P, :]
+            src = xt[:].rearrange("p g u r -> p g r u")
+            if on_vector:
+                nc.vector.tensor_copy(out=dst, in_=src)
+            else:
+                nc.scalar.copy(out=dst, in_=src)
+
+        def keys_quantise(b, g):
+            if g == 0:
+                kc = const.tile([P, 2 * K], U32, name="kc%d" % b, align_bytes=64)
+                ks = const.tile([P, 2 * K], U8, name="ks%d" % b, align_bytes=64)
+                kcodes[b], kscl[b] = kc, ks
+            nc.vector.quantize_mx(
+                out=kcodes[b][:, g * K : (g + 1) * K].bitcast(FP8X4),
+                scales=kscl[b][:, g * K : (g + 1) * K],
+                in_=gks[b][:, g * 4 * K : (g + 1) * 4 * K],
+            )
+
+        grps, codes, scls, lgs, outs = {}, {}, {}, {}, {}
+
+        def transpose_pair(i):
+            grp = gpool.tile([P, 2 * D], BF16, name="grp", align_bytes=64)
+            g32 = grp[:].bitcast(F32)
+            q32 = q_tiles[i // 2][:].bitcast(F32)
+            xts = []
+            for tl in range(2):
+                r = (i % 2) * 2 + tl
+                xt = ps_t.tile([P, 2, 2, P], F32, name="xt", tag="xt")
+                for w in range(4):
+                    col = r * (D // 2) + w * P
+                    nc.tensor.transpose(xt[:, w // 2, w % 2, :], q32[:, col : col + P], ident_f[:])
+                xts.append(xt)
+            for tl in range(2):
+                nc.scalar.copy(
+                    out=g32[:, tl * 512 : (tl + 1) * 512].rearrange("p (g r u) -> p g r u", g=2, u=2),
+                    in_=xts[tl][:].rearrange("p g u r -> p g r u"),
+                )
+            grps[i] = grp
+
+        def quantise_pair(i):
+            cd = cpool.tile([P, 512], U32, name="cd", align_bytes=64)
+            sc = cpool.tile([P, 512], U8, name="sc", align_bytes=64)
+            nc.vector.quantize_mx(out=cd[:].bitcast(FP8X4), scales=sc[:], in_=grps[i][:])
+            codes[i], scls[i] = cd, sc
+
+        def logits_pair(i):
+            b = (2 * i) // TILES_B
+            for tl in range(2):
+                lg = ps_l.tile([P, K], F32, name="lg")
+                for g in range(2):
+                    s = (tl * 2 + g) * P
+                    nc.tensor.matmul_mx(
+                        out=lg[:],
+                        lhsT=codes[i][:, s : s + P].bitcast(FP8X4),
+                        lhsT_scale=scls[i][:, s : s + P],
+                        rhs=kcodes[b][:, g * K : (g + 1) * K].bitcast(FP8X4),
+                        rhs_scale=kscl[b][:, g * K : (g + 1) * K],
+                        start=(g == 0),
+                        stop=(g == 1),
+                    )
+                lgs[2 * i + tl] = lg
+
+        def out_slice(t):
+            return outs[t // R][:, (t % R) * K : (t % R + 1) * K]
+
+        def mask_max_pair(i):
+            b = (2 * i) // TILES_B
+            if i % 2 == 0:
+                ot = opool.tile([P, R * K], F32, name="ot")
+                outs[i // 2] = ot
+            for tl in range(2):
+                t = 2 * i + tl
+                nc.vector.tensor_tensor(out=out_slice(t), in0=lgs[t][:], in1=caps[b][:], op=ALU.min)
+            if i >= 1:
+                finish_pair(i - 1, False)
+            for tl in range(2):
+                t = 2 * i + tl
+                nc.vector.tensor_reduce(out=negm[:, t : t + 1], in_=out_slice(t), axis=AX.X, op=ALU.max, negate=True)
+
+        def exp_pair(i):
+            for tl in range(2):
+                t = 2 * i + tl
+                nc.scalar.activation(
+                    out=out_slice(t), in_=out_slice(t), func=ACT.Exp,
+                    bias=negm[:, t : t + 1], scale=1.0, accum_out=zsum[:, t : t + 1],
+                )
+
+        def store(t0, n):
+            b, r = divmod(t0, TILES_B)
+            nc.sync.dma_start(
+                out=out_0[b].rearrange("(p r) k -> p (r k)", p=P)[:, r * K : (r + n) * K],
+                in_=outs[t0 // R][:, (t0 % R) * K : (t0 % R + n) * K],
+            )
+
+        def finish_pair(i, last):
+            if not last:
+                nc.vector.reciprocal(out=rz[:, 2 * i : 2 * i + 2], in_=zsum[:, 2 * i : 2 * i + 2])
+            for tl in range(2):
+                t = 2 * i + tl
+                if last:
+                    nc.vector.reciprocal(out=rz[:, t : t + 1], in_=zsum[:, t : t + 1])
+                    nc.vector.tensor_scalar_mul(out=out_slice(t), in0=out_slice(t), scalar1=rz[:, t : t + 1])
+                    store(t, 1)
+                else:
+                    nc.gpsimd.tensor_scalar(
+                        out=out_slice(t), in0=out_slice(t), scalar1=rz[:, t : t + 1], scalar2=0.0,
+                        op0=ALU.mult, op1=ALU.add,
+                    )
+            if i == N_PAIRS - 2:
+                store(2 * i, 2)
+            elif i % 2 == 1 and not last:
+                store(2 * i - 2, 4)
+
+        ctx.enter_context(tc.manual_schedule())
+        load_keys(0)
+        load_chunk(0, 2)
+        load_chunk(1)
+        load_chunk(2)
+        load_keys(1)
+        nc.sync.dma_start(out=t_bf[:], in_=temperature.partition_broadcast(P))
+        nc.sync.dma_start(out=b_bf[:], in_=bias.partition_broadcast(P))
+        for c in range(3, AHEAD):
+            load_chunk(c)
+
+        for t in range(4):
+            keys_transpose(0, t, t % 2 == 1)
+        keys_cap(0)
+        transpose_pair(0)
+        keys_quantise(0, 0)
+        keys_quantise(0, 1)
+        transpose_pair(1)
+        quantise_pair(0)
+        logits_pair(0)
+        for i in range(N_PAIRS):
+            if i % 2 == 0 and i // 2 + AHEAD < B * CHUNKS_B:
+                load_chunk(i // 2 + AHEAD)
+            if i + 2 < N_PAIRS:
+                transpose_pair(i + 2)
+            if 4 <= i < 8:
+                keys_transpose(1, i - 4, False)
+            if i == 8:
+                keys_cap(1)
+            if i + 1 < N_PAIRS:
+                quantise_pair(i + 1)
+            if 9 <= i < 11:
+                keys_quantise(1, i - 9)
+            if i == 12:
+                nc.vector.tensor_copy(out=t_f[:], in_=t_bf[:])
+                nc.vector.tensor_tensor(out=t_b[:], in0=t_bf[:], in1=b_bf[:], op=ALU.mult)
+            mask_max_pair(i)
+            if i + 1 < N_PAIRS:
+                logits_pair(i + 1)
+            exp_pair(i)
+        finish_pair(N_PAIRS - 1, True)
+
+        lse = const.tile([P, N_TILES], F32, name="lse")
+        conf = const.tile([P, N_TILES], F32, name="conf")
+        nc.scalar.activation(out=lse[:], in_=zsum[:], func=ACT.Ln)
+        nc.vector.tensor_tensor(out=lse[:], in0=lse[:], in1=negm[:], op=ALU.subtract)
+        nc.scalar.activation(out=conf[:], in_=lse[:], func=ACT.Sigmoid, bias=t_b[:], scale=t_f[:])
+        nc.sync.dma_start(
+            out=out_1.rearrange("b (p r) -> p b r", p=P),
+            in_=conf[:].rearrange("p (b r) -> p b r", b=B),
+        )

@@ -56,11 +56,12 @@ def tile_contentattention_t_kernel(tc, queries, keys, temperature, bias, out_0, 
 
         q_tiles = {}
 
-        def load_keys(b):
-            for h in range(2):
+        def load_keys(b, pieces):
+            n = 4 // pieces
+            for h in range(pieces):
                 nc.sync.dma_start(
-                    out=k_sb[:, (b * 4 + 2 * h) * D : (b * 4 + 2 * h + 2) * D].rearrange("p (t d) -> p t d", t=2),
-                    in_=keys[b][2 * h * P : (2 * h + 2) * P, :].rearrange("(t p) d -> p t d", p=P),
+                    out=k_sb[:, (b * 4 + n * h) * D : (b * 4 + n * h + n) * D].rearrange("p (t d) -> p t d", t=n),
+                    in_=keys[b][n * h * P : (n * h + n) * P, :].rearrange("(t p) d -> p t d", p=P),
                 )
 
         def load_chunk(c, pieces=1):
@@ -112,20 +113,21 @@ def tile_contentattention_t_kernel(tc, queries, keys, temperature, bias, out_0, 
             else:
                 nc.scalar.copy(out=dst, in_=src)
 
-        def keys_quantise(b, g):
-            if g == 0:
+        def keys_quantise(b, g, j0, n):
+            if b not in kcodes:
                 kc = const.tile([P, 2 * K], U32, name="kc%d" % b, align_bytes=64)
                 ks = const.tile([P, 2 * K], U8, name="ks%d" % b, align_bytes=64)
                 kcodes[b], kscl[b] = kc, ks
+            c0 = g * K + j0
             nc.vector.quantize_mx(
-                out=kcodes[b][:, g * K : (g + 1) * K].bitcast(FP8X4),
-                scales=kscl[b][:, g * K : (g + 1) * K],
-                in_=gks[b][:, g * 4 * K : (g + 1) * 4 * K],
+                out=kcodes[b][:, c0 : c0 + n].bitcast(FP8X4),
+                scales=kscl[b][:, c0 : c0 + n],
+                in_=gks[b][:, 4 * c0 : 4 * (c0 + n)],
             )
 
         grps, codes, scls, lgs, outs = {}, {}, {}, {}, {}
 
-        def transpose_pair(i):
+        def transpose_pair(i, share=False):
             grp = gpool.tile([P, 2 * D], BF16, name="grp", align_bytes=64)
             g32 = grp[:].bitcast(F32)
             q32 = q_tiles[i // 2][:].bitcast(F32)
@@ -138,10 +140,12 @@ def tile_contentattention_t_kernel(tc, queries, keys, temperature, bias, out_0, 
                     nc.tensor.transpose(xt[:, w // 2, w % 2, :], q32[:, col : col + P], ident_f[:])
                 xts.append(xt)
             for tl in range(2):
-                nc.scalar.copy(
-                    out=g32[:, tl * 512 : (tl + 1) * 512].rearrange("p (g r u) -> p g r u", g=2, u=2),
-                    in_=xts[tl][:].rearrange("p g u r -> p g r u"),
-                )
+                dst = g32[:, tl * 512 : (tl + 1) * 512].rearrange("p (g r u) -> p g r u", g=2, u=2)
+                src = xts[tl][:].rearrange("p g u r -> p g r u")
+                if share and tl == 1:
+                    nc.vector.tensor_copy(out=dst, in_=src)
+                else:
+                    nc.scalar.copy(out=dst, in_=src)
             grps[i] = grp
 
         def quantise_pair(i):
@@ -178,8 +182,8 @@ def tile_contentattention_t_kernel(tc, queries, keys, temperature, bias, out_0, 
             for tl in range(2):
                 t = 2 * i + tl
                 nc.vector.tensor_tensor(out=out_slice(t), in0=lgs[t][:], in1=caps[b][:], op=ALU.min)
-            if i >= 1:
-                finish_pair(i - 1, False)
+                if i >= 1 and tl == 0:
+                    finish_pair(i - 1, False)
             for tl in range(2):
                 t = 2 * i + tl
                 nc.vector.tensor_reduce(out=negm[:, t : t + 1], in_=out_slice(t), axis=AX.X, op=ALU.max, negate=True)
@@ -219,11 +223,11 @@ def tile_contentattention_t_kernel(tc, queries, keys, temperature, bias, out_0, 
                 store(2 * i - 2, 4)
 
         ctx.enter_context(tc.manual_schedule())
-        load_keys(0)
-        load_chunk(0, 2)
+        load_keys(0, 4)
+        load_chunk(0, 4)
         load_chunk(1)
         load_chunk(2)
-        load_keys(1)
+        load_keys(1, 2)
         nc.sync.dma_start(out=t_bf[:], in_=temperature.partition_broadcast(P))
         nc.sync.dma_start(out=b_bf[:], in_=bias.partition_broadcast(P))
         for c in range(3, AHEAD):
@@ -231,10 +235,13 @@ def tile_contentattention_t_kernel(tc, queries, keys, temperature, bias, out_0, 
 
         for t in range(4):
             keys_transpose(0, t, t % 2 == 1)
+            if t >= 1:
+                keys_quantise(0, 0, (t - 1) * P, P)
+                keys_quantise(0, 1, (t - 1) * P, P)
         keys_cap(0)
-        transpose_pair(0)
-        keys_quantise(0, 0)
-        keys_quantise(0, 1)
+        keys_quantise(0, 0, 3 * P, P)
+        keys_quantise(0, 1, 3 * P, P)
+        transpose_pair(0, True)
         transpose_pair(1)
         quantise_pair(0)
         logits_pair(0)
@@ -250,7 +257,7 @@ def tile_contentattention_t_kernel(tc, queries, keys, temperature, bias, out_0, 
             if i + 1 < N_PAIRS:
                 quantise_pair(i + 1)
             if 9 <= i < 11:
-                keys_quantise(1, i - 9)
+                keys_quantise(1, i - 9, 0, K)
             if i == 12:
                 nc.vector.tensor_copy(out=t_f[:], in_=t_bf[:])
                 nc.vector.tensor_tensor(out=t_b[:], in0=t_bf[:], in1=b_bf[:], op=ALU.mult)

@@ -77,7 +77,7 @@ def tile_contentattention_t_kernel(tc, queries, keys, temperature, bias, out_0, 
 
         kcodes, kscl, caps = {}, {}, {}
 
-        gks = {}
+        gks, mbs = {}, {}
 
         def keys_cap(b):
             capv = const.tile([P, 4], BF16, name="capv%d" % b)
@@ -96,6 +96,11 @@ def tile_contentattention_t_kernel(tc, queries, keys, temperature, bias, out_0, 
             cap = const.tile([P, K], F32, name="cap%d" % b)
             nc.scalar.copy(out=cap[:], in_=cap_ps[:])
             caps[b] = cap
+
+        def keys_addend(b):
+            mb = const.tile([P, K], F32, name="mb%d" % b)
+            nc.vector.tensor_scalar_min(out=mb[:], in0=caps[b][:], scalar1=0.0)
+            mbs[b] = mb
 
         def keys_transpose(b, t, on_vector):
             if t == 0:
@@ -174,19 +179,25 @@ def tile_contentattention_t_kernel(tc, queries, keys, temperature, bias, out_0, 
         def out_slice(t):
             return outs[t // R][:, (t % R) * K : (t % R + 1) * K]
 
-        def mask_max_pair(i):
-            b = (2 * i) // TILES_B
-            if i % 2 == 0:
+        def by_scalar(t):
+            return t >= R and t % R == R - 1
+
+        def need_out(t):
+            if t // R not in outs:
                 ot = opool.tile([P, R * K], F32, name="ot")
-                outs[i // 2] = ot
-            for tl in range(2):
-                t = 2 * i + tl
-                nc.vector.tensor_tensor(out=out_slice(t), in0=lgs[t][:], in1=caps[b][:], op=ALU.min)
-                if i >= 1 and tl == 0:
-                    finish_pair(i - 1, False)
-            for tl in range(2):
-                t = 2 * i + tl
-                nc.vector.tensor_reduce(out=negm[:, t : t + 1], in_=out_slice(t), axis=AX.X, op=ALU.max, negate=True)
+                outs[t // R] = ot
+
+        def mask_vector(t):
+            need_out(t)
+            nc.vector.tensor_tensor(out=out_slice(t), in0=lgs[t][:], in1=caps[t // TILES_B][:], op=ALU.min)
+
+        def mask_scalar_gpsimd(t):
+            need_out(t)
+            nc.scalar.copy(out=out_slice(t), in_=lgs[t][:])
+            nc.gpsimd.tensor_tensor(out=out_slice(t), in0=out_slice(t), in1=mbs[t // TILES_B][:], op=ALU.add)
+
+        def row_max(t):
+            nc.vector.tensor_reduce(out=negm[:, t : t + 1], in_=out_slice(t), axis=AX.X, op=ALU.max, negate=True)
 
         def exp_pair(i):
             for tl in range(2):
@@ -258,12 +269,24 @@ def tile_contentattention_t_kernel(tc, queries, keys, temperature, bias, out_0, 
                 quantise_pair(i + 1)
             if 9 <= i < 11:
                 keys_quantise(1, i - 9, 0, K)
+            if i == 1 or i == 11:
+                keys_addend(i // 11)
             if i == 12:
                 nc.vector.tensor_copy(out=t_f[:], in_=t_bf[:])
                 nc.vector.tensor_tensor(out=t_b[:], in0=t_bf[:], in1=b_bf[:], op=ALU.mult)
-            mask_max_pair(i)
+            mine = [t for t in (2 * i, 2 * i + 1) if not by_scalar(t)]
+            theirs = [t for t in (2 * i, 2 * i + 1) if by_scalar(t)]
+            for t in mine:
+                mask_vector(t)
             if i + 1 < N_PAIRS:
                 logits_pair(i + 1)
+                for t in (2 * i + 2, 2 * i + 3):
+                    if by_scalar(t):
+                        mask_scalar_gpsimd(t)
+            if i >= 1:
+                finish_pair(i - 1, False)
+            for t in mine + theirs:
+                row_max(t)
             exp_pair(i)
         finish_pair(N_PAIRS - 1, True)
 

@@ -49,6 +49,9 @@ def tile_contentattention_t_kernel(tc, queries, keys, temperature, bias, out_0, 
         zsum = const.tile([P, N_TILES], F32, name="zsum")
         negm = const.tile([P, N_TILES], F32, name="negm")
         rz = const.tile([P, N_TILES], F32, name="rz")
+        rz_last = const.tile([P, 2], F32, name="rz_last")
+        neg_one = const.tile([P, 2], F32, name="neg_one")
+        nc.vector.memset(neg_one[:], -1.0)
         t_bf = const.tile([P, 1], BF16, name="t_bf")
         b_bf = const.tile([P, 1], BF16, name="b_bf")
         t_f = const.tile([P, 1], F32, name="t_f")
@@ -56,12 +59,11 @@ def tile_contentattention_t_kernel(tc, queries, keys, temperature, bias, out_0, 
 
         q_tiles = {}
 
-        def load_keys(b, pieces):
-            n = 4 // pieces
-            for h in range(pieces):
+        def load_keys(b):
+            for h in range(2):
                 nc.sync.dma_start(
-                    out=k_sb[:, (b * 4 + n * h) * D : (b * 4 + n * h + n) * D].rearrange("p (t d) -> p t d", t=n),
-                    in_=keys[b][n * h * P : (n * h + n) * P, :].rearrange("(t p) d -> p t d", p=P),
+                    out=k_sb[:, (b * 4 + 2 * h) * D : (b * 4 + 2 * h + 2) * D].rearrange("p (t d) -> p t d", t=2),
+                    in_=keys[b][2 * h * P : (2 * h + 2) * P, :].rearrange("(t p) d -> p t d", p=P),
                 )
 
         def load_chunk(c, pieces=1):
@@ -77,7 +79,7 @@ def tile_contentattention_t_kernel(tc, queries, keys, temperature, bias, out_0, 
 
         kcodes, kscl, caps = {}, {}, {}
 
-        gks, mbs = {}, {}
+        gks = {}
 
         def keys_cap(b):
             capv = const.tile([P, 4], BF16, name="capv%d" % b)
@@ -97,11 +99,6 @@ def tile_contentattention_t_kernel(tc, queries, keys, temperature, bias, out_0, 
             nc.scalar.copy(out=cap[:], in_=cap_ps[:])
             caps[b] = cap
 
-        def keys_addend(b):
-            mb = const.tile([P, K], F32, name="mb%d" % b)
-            nc.vector.tensor_scalar_min(out=mb[:], in0=caps[b][:], scalar1=0.0)
-            mbs[b] = mb
-
         def keys_transpose(b, t, on_vector):
             if t == 0:
                 gk = const.tile([P, 2 * K * 4], BF16, name="gk%d" % b, align_bytes=64)
@@ -118,21 +115,20 @@ def tile_contentattention_t_kernel(tc, queries, keys, temperature, bias, out_0, 
             else:
                 nc.scalar.copy(out=dst, in_=src)
 
-        def keys_quantise(b, g, j0, n):
-            if b not in kcodes:
+        def keys_quantise(b, g):
+            if g == 0:
                 kc = const.tile([P, 2 * K], U32, name="kc%d" % b, align_bytes=64)
                 ks = const.tile([P, 2 * K], U8, name="ks%d" % b, align_bytes=64)
                 kcodes[b], kscl[b] = kc, ks
-            c0 = g * K + j0
             nc.vector.quantize_mx(
-                out=kcodes[b][:, c0 : c0 + n].bitcast(FP8X4),
-                scales=kscl[b][:, c0 : c0 + n],
-                in_=gks[b][:, 4 * c0 : 4 * (c0 + n)],
+                out=kcodes[b][:, g * K : (g + 1) * K].bitcast(FP8X4),
+                scales=kscl[b][:, g * K : (g + 1) * K],
+                in_=gks[b][:, g * 4 * K : (g + 1) * 4 * K],
             )
 
         grps, codes, scls, lgs, outs = {}, {}, {}, {}, {}
 
-        def transpose_pair(i, share=False):
+        def transpose_pair(i):
             grp = gpool.tile([P, 2 * D], BF16, name="grp", align_bytes=64)
             g32 = grp[:].bitcast(F32)
             q32 = q_tiles[i // 2][:].bitcast(F32)
@@ -145,12 +141,10 @@ def tile_contentattention_t_kernel(tc, queries, keys, temperature, bias, out_0, 
                     nc.tensor.transpose(xt[:, w // 2, w % 2, :], q32[:, col : col + P], ident_f[:])
                 xts.append(xt)
             for tl in range(2):
-                dst = g32[:, tl * 512 : (tl + 1) * 512].rearrange("p (g r u) -> p g r u", g=2, u=2)
-                src = xts[tl][:].rearrange("p g u r -> p g r u")
-                if share and tl == 1:
-                    nc.vector.tensor_copy(out=dst, in_=src)
-                else:
-                    nc.scalar.copy(out=dst, in_=src)
+                nc.scalar.copy(
+                    out=g32[:, tl * 512 : (tl + 1) * 512].rearrange("p (g r u) -> p g r u", g=2, u=2),
+                    in_=xts[tl][:].rearrange("p g u r -> p g r u"),
+                )
             grps[i] = grp
 
         def quantise_pair(i):
@@ -179,25 +173,19 @@ def tile_contentattention_t_kernel(tc, queries, keys, temperature, bias, out_0, 
         def out_slice(t):
             return outs[t // R][:, (t % R) * K : (t % R + 1) * K]
 
-        def by_scalar(t):
-            return t >= R and t % R == R - 1
-
-        def need_out(t):
-            if t // R not in outs:
+        def mask_max_pair(i):
+            b = (2 * i) // TILES_B
+            if i % 2 == 0:
                 ot = opool.tile([P, R * K], F32, name="ot")
-                outs[t // R] = ot
-
-        def mask_vector(t):
-            need_out(t)
-            nc.vector.tensor_tensor(out=out_slice(t), in0=lgs[t][:], in1=caps[t // TILES_B][:], op=ALU.min)
-
-        def mask_scalar_gpsimd(t):
-            need_out(t)
-            nc.scalar.copy(out=out_slice(t), in_=lgs[t][:])
-            nc.gpsimd.tensor_tensor(out=out_slice(t), in0=out_slice(t), in1=mbs[t // TILES_B][:], op=ALU.add)
-
-        def row_max(t):
-            nc.vector.tensor_reduce(out=negm[:, t : t + 1], in_=out_slice(t), axis=AX.X, op=ALU.max, negate=True)
+                outs[i // 2] = ot
+            for tl in range(2):
+                t = 2 * i + tl
+                nc.vector.tensor_tensor(out=out_slice(t), in0=lgs[t][:], in1=caps[b][:], op=ALU.min)
+            if i >= 1:
+                finish_pair(i - 1, False)
+            for tl in range(2):
+                t = 2 * i + tl
+                nc.vector.tensor_reduce(out=negm[:, t : t + 1], in_=out_slice(t), axis=AX.X, op=ALU.max, negate=True)
 
         def exp_pair(i):
             for tl in range(2):
@@ -216,12 +204,12 @@ def tile_contentattention_t_kernel(tc, queries, keys, temperature, bias, out_0, 
 
         def finish_pair(i, last):
             if not last:
-                nc.vector.reciprocal(out=rz[:, 2 * i : 2 * i + 2], in_=zsum[:, 2 * i : 2 * i + 2])
+                nc.gpsimd.tensor_tensor(out=rz[:, 2 * i : 2 * i + 2], in0=zsum[:, 2 * i : 2 * i + 2], in1=neg_one[:], op=ALU.pow)
             for tl in range(2):
                 t = 2 * i + tl
                 if last:
-                    nc.vector.reciprocal(out=rz[:, t : t + 1], in_=zsum[:, t : t + 1])
-                    nc.vector.tensor_scalar_mul(out=out_slice(t), in0=out_slice(t), scalar1=rz[:, t : t + 1])
+                    nc.vector.reciprocal(out=rz_last[:, tl : tl + 1], in_=zsum[:, t : t + 1])
+                    nc.vector.tensor_scalar_mul(out=out_slice(t), in0=out_slice(t), scalar1=rz_last[:, tl : tl + 1])
                     store(t, 1)
                 else:
                     nc.gpsimd.tensor_scalar(
@@ -234,11 +222,11 @@ def tile_contentattention_t_kernel(tc, queries, keys, temperature, bias, out_0, 
                 store(2 * i - 2, 4)
 
         ctx.enter_context(tc.manual_schedule())
-        load_keys(0, 4)
-        load_chunk(0, 4)
+        load_keys(0)
+        load_chunk(0, 2)
         load_chunk(1)
         load_chunk(2)
-        load_keys(1, 2)
+        load_keys(1)
         nc.sync.dma_start(out=t_bf[:], in_=temperature.partition_broadcast(P))
         nc.sync.dma_start(out=b_bf[:], in_=bias.partition_broadcast(P))
         for c in range(3, AHEAD):
@@ -246,13 +234,10 @@ def tile_contentattention_t_kernel(tc, queries, keys, temperature, bias, out_0, 
 
         for t in range(4):
             keys_transpose(0, t, t % 2 == 1)
-            if t >= 1:
-                keys_quantise(0, 0, (t - 1) * P, P)
-                keys_quantise(0, 1, (t - 1) * P, P)
         keys_cap(0)
-        keys_quantise(0, 0, 3 * P, P)
-        keys_quantise(0, 1, 3 * P, P)
-        transpose_pair(0, True)
+        transpose_pair(0)
+        keys_quantise(0, 0)
+        keys_quantise(0, 1)
         transpose_pair(1)
         quantise_pair(0)
         logits_pair(0)
@@ -268,25 +253,13 @@ def tile_contentattention_t_kernel(tc, queries, keys, temperature, bias, out_0, 
             if i + 1 < N_PAIRS:
                 quantise_pair(i + 1)
             if 9 <= i < 11:
-                keys_quantise(1, i - 9, 0, K)
-            if i == 1 or i == 11:
-                keys_addend(i // 11)
+                keys_quantise(1, i - 9)
             if i == 12:
                 nc.vector.tensor_copy(out=t_f[:], in_=t_bf[:])
                 nc.vector.tensor_tensor(out=t_b[:], in0=t_bf[:], in1=b_bf[:], op=ALU.mult)
-            mine = [t for t in (2 * i, 2 * i + 1) if not by_scalar(t)]
-            theirs = [t for t in (2 * i, 2 * i + 1) if by_scalar(t)]
-            for t in mine:
-                mask_vector(t)
+            mask_max_pair(i)
             if i + 1 < N_PAIRS:
                 logits_pair(i + 1)
-                for t in (2 * i + 2, 2 * i + 3):
-                    if by_scalar(t):
-                        mask_scalar_gpsimd(t)
-            if i >= 1:
-                finish_pair(i - 1, False)
-            for t in mine + theirs:
-                row_max(t)
             exp_pair(i)
         finish_pair(N_PAIRS - 1, True)
 

from contextlib import ExitStack

import concourse.mybir as mybir
from concourse.masks import make_identity

F32 = mybir.dt.float32
BF16 = mybir.dt.bfloat16
U32 = mybir.dt.uint32
U8 = mybir.dt.uint8
FP8X4 = mybir.dt.float8_e4m3fn_x4
ALU = mybir.AluOpType
ACT = mybir.ActivationFunctionType
AX = mybir.AxisListType

P = 128
B, Q, K, D = 2, 4096, 512, 1024
FLOPS = 2 * B * Q * K * D
R = 4
TILES_B = Q // P
CHUNKS_B = TILES_B // R
N_TILES = B * TILES_B
N_PAIRS = N_TILES // 2
BIG = 2.0 ** 120
AHEAD = 8


def tile_contentattention_t_kernel(tc, queries, keys, temperature, bias, out_0, out_1):
    nc = tc.nc
    with ExitStack() as ctx:
        const = ctx.enter_context(tc.tile_pool(name="const", bufs=1))
        qpool = ctx.enter_context(tc.tile_pool(name="qpool", bufs=10))
        gpool = ctx.enter_context(tc.tile_pool(name="gpool", bufs=3))
        cpool = ctx.enter_context(tc.tile_pool(name="cpool", bufs=4))
        opool = ctx.enter_context(tc.tile_pool(name="opool", bufs=4))
        ps_t = ctx.enter_context(tc.psum_pool(name="ps_t", bufs=4))
        ps_l = ctx.enter_context(tc.psum_pool(name="ps_l", bufs=4))

        one = const.tile([P, 1], F32, name="one")
        junk = const.tile([P, 1], F32, name="junk")
        nc.vector.memset(one[:], 1.0)
        nc.scalar.activation(out=junk[:], in_=one[:], func=ACT.Exp)
        ident_f = const.tile([P, P], F32, name="ident_f")
        ident_b = const.tile([P, P], BF16, name="ident_b")
        make_identity(nc, ident_f[:])
        make_identity(nc, ident_b[:])

        k_sb = const.tile([P, B * 4 * D], BF16, name="k_sb")
        k32 = k_sb[:].bitcast(F32)
        zsum = const.tile([P, N_TILES], F32, name="zsum")
        negm = const.tile([P, N_TILES], F32, name="negm")
        rz = const.tile([P, N_TILES], F32, name="rz")
        rz_last = const.tile([P, 2], F32, name="rz_last")
        neg_one = const.tile([P, 2], F32, name="neg_one")
        nc.vector.memset(neg_one[:], -1.0)
        t_bf = const.tile([P, 1], BF16, name="t_bf")
        b_bf = const.tile([P, 1], BF16, name="b_bf")
        t_f = const.tile([P, 1], F32, name="t_f")
        t_b = const.tile([P, 1], F32, name="t_b")

        q_tiles = {}

        def load_keys(b):
            for h in range(2):
                nc.sync.dma_start(
                    out=k_sb[:, (b * 4 + 2 * h) * D : (b * 4 + 2 * h + 2) * D].rearrange("p (t d) -> p t d", t=2),
                    in_=keys[b][2 * h * P : (2 * h + 2) * P, :].rearrange("(t p) d -> p t d", p=P),
                )

        def load_chunk(c, pieces=1):
            b, cc = divmod(c, CHUNKS_B)
            q_sb = qpool.tile([P, R * D], BF16, name="q_sb")
            w = R * D // pieces
            for h in range(pieces):
                nc.sync.dma_start(
                    out=q_sb[:, h * w : (h + 1) * w],
                    in_=queries[b].rearrange("(p r) d -> p (r d)", p=P)[:, cc * R * D + h * w : cc * R * D + (h + 1) * w],
                )
            q_tiles[c] = q_sb

        kcodes, kscl, caps = {}, {}, {}

        gks = {}

        def keys_cap(b):
            capv = const.tile([P, 4], BF16, name="capv%d" % b)
            first = k_sb[:, b * 4 * D : (b + 1) * 4 * D].rearrange("p (t d) -> p t d", t=4)[:, :, 0:1]
            nc.vector.tensor_scalar(out=capv[:].rearrange("p (t o) -> p t o", o=1), in0=first, scalar1=0.0, scalar2=-2.0 * BIG, op0=ALU.is_equal, op1=ALU.mult)
            nc.vector.tensor_scalar_add(out=capv[:], in0=capv[:], scalar1=BIG)
            cap_ps = ps_t.tile([P, K], F32, name="cap_ps", tag="xt")
            for t in range(4):
                nc.tensor.matmul(
                    out=cap_ps[:, t * P : (t + 1) * P],
                    lhsT=capv[:, t : t + 1].to_broadcast([P, P]),
                    rhs=ident_b[:],
                    start=True,
                    stop=True,
                )
            cap = const.tile([P, K], F32, name="cap%d" % b)
            nc.scalar.copy(out=cap[:], in_=cap_ps[:])
            caps[b] = cap

        def keys_transpose(b, t, on_vector):
            if t == 0:
                gk = const.tile([P, 2 * K * 4], BF16, name="gk%d" % b, align_bytes=64)
                gks[b] = gk
            gk32 = gks[b][:].bitcast(F32).rearrange("p (g j u) -> p g j u", g=2, u=2)
            xt = ps_t.tile([P, 2, 2, P], F32, name="xt", tag="xt")
            for w in range(4):
                col = (b * 4 + t) * (D // 2) + w * P
                nc.tensor.transpose(xt[:, w // 2, w % 2, :], k32[:, col : col + P], ident_f[:])
            dst = gk32[:, :, t * P : (t + 1) * P, :]
            src = xt[:].rearrange("p g u r -> p g r u")
            if on_vector:
                nc.vector.tensor_copy(out=dst, in_=src)
            else:
                nc.scalar.copy(out=dst, in_=src)

        def keys_quantise(b, g):
            if g == 0:
                kc = const.tile([P, 2 * K], U32, name="kc%d" % b, align_bytes=64)
                ks = const.tile([P, 2 * K], U8, name="ks%d" % b, align_bytes=64)
                kcodes[b], kscl[b] = kc, ks
            nc.vector.quantize_mx(
                out=kcodes[b][:, g * K : (g + 1) * K].bitcast(FP8X4),
                scales=kscl[b][:, g * K : (g + 1) * K],
                in_=gks[b][:, g * 4 * K : (g + 1) * 4 * K],
            )

        grps, codes, scls, lgs, outs = {}, {}, {}, {}, {}

        def transpose_pair(i):
            grp = gpool.tile([P, 2 * D], BF16, name="grp", align_bytes=64)
            g32 = grp[:].bitcast(F32)
            q32 = q_tiles[i // 2][:].bitcast(F32)
            xts = []
            for tl in range(2):
                r = (i % 2) * 2 + tl
                xt = ps_t.tile([P, 2, 2, P], F32, name="xt", tag="xt")
                for w in range(4):
                    col = r * (D // 2) + w * P
                    nc.tensor.transpose(xt[:, w // 2, w % 2, :], q32[:, col : col + P], ident_f[:])
                xts.append(xt)
            for tl in range(2):
                nc.scalar.copy(
                    out=g32[:, tl * 512 : (tl + 1) * 512].rearrange("p (g r u) -> p g r u", g=2, u=2),
                    in_=xts[tl][:].rearrange("p g u r -> p g r u"),
                )
            grps[i] = grp

        def quantise_pair(i):
            cd = cpool.tile([P, 512], U32, name="cd", align_bytes=64)
            sc = cpool.tile([P, 512], U8, name="sc", align_bytes=64)
            nc.vector.quantize_mx(out=cd[:].bitcast(FP8X4), scales=sc[:], in_=grps[i][:])
            codes[i], scls[i] = cd, sc

        def logits_pair(i):
            b = (2 * i) // TILES_B
            for tl in range(2):
                lg = ps_l.tile([P, K], F32, name="lg")
                for g in range(2):
                    s = (tl * 2 + g) * P
                    nc.tensor.matmul_mx(
                        out=lg[:],
                        lhsT=codes[i][:, s : s + P].bitcast(FP8X4),
                        lhsT_scale=scls[i][:, s : s + P],
                        rhs=kcodes[b][:, g * K : (g + 1) * K].bitcast(FP8X4),
                        rhs_scale=kscl[b][:, g * K : (g + 1) * K],
                        start=(g == 0),
                        stop=(g == 1),
                    )
                lgs[2 * i + tl] = lg

        def out_slice(t):
            return outs[t // R][:, (t % R) * K : (t % R + 1) * K]

        def mask_max_pair(i):
            b = (2 * i) // TILES_B
            if i % 2 == 0:
                ot = opool.tile([P, R * K], F32, name="ot")
                outs[i // 2] = ot
            for tl in range(2):
                t = 2 * i + tl
                nc.vector.tensor_tensor(out=out_slice(t), in0=lgs[t][:], in1=caps[b][:], op=ALU.min)
            if i >= 1:
                finish_pair(i - 1, False)
            for tl in range(2):
                t = 2 * i + tl
                nc.vector.tensor_reduce(out=negm[:, t : t + 1], in_=out_slice(t), axis=AX.X, op=ALU.max, negate=True)

        def exp_pair(i):
            for tl in range(2):
                t = 2 * i + tl
                nc.scalar.activation(
                    out=out_slice(t), in_=out_slice(t), func=ACT.Exp,
                    bias=negm[:, t : t + 1], scale=1.0, accum_out=zsum[:, t : t + 1],
                )

        def store(t0, n):
            b, r = divmod(t0, TILES_B)
            nc.sync.dma_start(
                out=out_0[b].rearrange("(p r) k -> p (r k)", p=P)[:, r * K : (r + n) * K],
                in_=outs[t0 // R][:, (t0 % R) * K : (t0 % R + n) * K],
            )

        def finish_pair(i, last):
            if not last:
                nc.gpsimd.tensor_tensor(out=rz[:, 2 * i : 2 * i + 2], in0=zsum[:, 2 * i : 2 * i + 2], in1=neg_one[:], op=ALU.pow)
            for tl in range(2):
                t = 2 * i + tl
                if last:
                    nc.vector.reciprocal(out=rz_last[:, tl : tl + 1], in_=zsum[:, t : t + 1])
                    nc.vector.tensor_scalar_mul(out=out_slice(t), in0=out_slice(t), scalar1=rz_last[:, tl : tl + 1])
                    store(t, 1)
                else:
                    nc.gpsimd.tensor_scalar(
                        out=out_slice(t), in0=out_slice(t), scalar1=rz[:, t : t + 1], scalar2=0.0,
                        op0=ALU.mult, op1=ALU.add,
                    )
            if i == N_PAIRS - 2:
                store(2 * i, 2)
            elif i % 2 == 1 and not last:
                store(2 * i - 2, 4)

        ctx.enter_context(tc.manual_schedule())
        load_keys(0)
        load_chunk(0, 2)
        load_chunk(1)
        load_chunk(2)
        load_keys(1)
        nc.sync.dma_start(out=t_bf[:], in_=temperature.partition_broadcast(P))
        nc.sync.dma_start(out=b_bf[:], in_=bias.partition_broadcast(P))
        for c in range(3, AHEAD):
            load_chunk(c)

        for t in range(4):
            keys_transpose(0, t, t % 2 == 1)
        keys_cap(0)
        transpose_pair(0)
        keys_quantise(0, 0)
        keys_quantise(0, 1)
        transpose_pair(1)
        quantise_pair(0)
        logits_pair(0)
        for i in range(N_PAIRS):
            if i % 2 == 0 and i // 2 + AHEAD < B * CHUNKS_B:
                load_chunk(i // 2 + AHEAD)
            if i + 2 < N_PAIRS:
                transpose_pair(i + 2)
            if 4 <= i < 8:
                keys_transpose(1, i - 4, False)
            if i == 8:
                keys_cap(1)
            if i + 1 < N_PAIRS:
                quantise_pair(i + 1)
            if 9 <= i < 11:
                keys_quantise(1, i - 9)
            if i == 12:
                nc.vector.tensor_copy(out=t_f[:], in_=t_bf[:])
                nc.vector.tensor_tensor(out=t_b[:], in0=t_bf[:], in1=b_bf[:], op=ALU.mult)
            mask_max_pair(i)
            if i + 1 < N_PAIRS:
                logits_pair(i + 1)
            exp_pair(i)
        finish_pair(N_PAIRS - 1, True)

        lse = const.tile([P, N_TILES], F32, name="lse")
        conf = const.tile([P, N_TILES], F32, name="conf")
        nc.scalar.activation(out=lse[:], in_=zsum[:], func=ACT.Ln)
        nc.vector.tensor_tensor(out=lse[:], in0=lse[:], in1=negm[:], op=ALU.subtract)
        nc.scalar.activation(out=conf[:], in_=lse[:], func=ACT.Sigmoid, bias=t_b[:], scale=t_f[:])
        nc.sync.dma_start(
            out=out_1.rearrange("b (p r) -> p b r", p=P),
            in_=conf[:].rearrange("p (b r) -> p b r", b=B),
        )
